import numpy as np
import ml_dtypes


def mxq(x, axis, fmt="e4m3"):
    dtype, down = {"e4m3": (ml_dtypes.float8_e4m3fn, 7), "e5m2": (ml_dtypes.float8_e5m2, 14)}[fmt]
    v = np.moveaxis(np.asarray(x, np.float32).astype(ml_dtypes.bfloat16).astype(np.float64), axis, -1)
    blocks = v.reshape(v.shape[:-1] + (-1, 32))
    amax = np.abs(blocks).max(-1, keepdims=True)
    byte = np.maximum(np.where(amax > 0, np.frexp(amax)[1] - 1 + 127, 0) - down, 1)
    scale = np.exp2(byte - 127.0)
    codes = (blocks / scale).astype(np.float32).astype(dtype).astype(np.float64)
    return np.moveaxis((codes * scale).reshape(v.shape), -1, axis)


WIDE = False


def mx_kscale(k):
    if not WIDE:
        return np.ones(k)
    levels = np.array([10, -10, 5, -5, 0])
    a = np.random.permutation(np.resize(levels, k // 512 * 4)).reshape(k // 512, 4)
    idx = np.arange(k)
    return np.exp2(a[idx // 512, idx % 128 // 32])


BF16 = ml_dtypes.bfloat16


def bf(x):
    return np.asarray(x, np.float32).astype(BF16)


def f64(x):
    return np.asarray(x).astype(np.float64)


E2M1 = np.array([0.0, 0.5, 1.0, 1.5, 2.0, 3.0, 4.0, 6.0, -0.0, -0.5, -1.0, -1.5, -2.0, -3.0, -4.0, -6.0])


def pack_weight(w, fmt):
    k, n = w.shape
    w = f64(bf(w)).reshape(k // 32, 32, n)
    amax = np.abs(w).max(1)
    if fmt == "e4m3":
        byte = np.frexp(amax)[1] - 1 + 127 - 7
    else:
        mant, ex = np.frexp(amax / 6.0)
        byte = np.where(mant > 0.5, ex, ex - 1) + 127
    byte = np.clip(np.where(amax > 0, byte, 1), 1, 254)
    scaled = (w * np.exp2(127.0 - byte)[:, None, :]).reshape(k, n).astype(np.float32)
    by_word = np.ascontiguousarray(scaled.reshape(k // 512, 128, 4, n).transpose(0, 1, 3, 2))
    if fmt == "e4m3":
        words = by_word.astype(ml_dtypes.float8_e4m3fn).view(np.uint8)
    else:
        c = by_word.astype(ml_dtypes.float4_e2m1fn).view(np.uint8) & 0xF
        words = c[..., 0::2] | (c[..., 1::2] << 4)
    return np.ascontiguousarray(words), np.ascontiguousarray(byte.astype(np.uint8).reshape(k // 512, 16, n))


def unpack_weight(words, scales, fmt):
    g, p, n, _ = words.shape
    if fmt == "e4m3":
        vals = np.ascontiguousarray(words).view(ml_dtypes.float8_e4m3fn).astype(np.float64)
    else:
        nib = np.empty((g, p, n, 4), np.uint8)
        nib[..., 0::2] = words & 0xF
        nib[..., 1::2] = words >> 4
        vals = E2M1[nib]
    vals = vals * np.repeat(np.exp2(scales.astype(np.float64) - 127.0), 8, axis=1)[..., None]
    return vals.transpose(0, 1, 3, 2).reshape(g * 512, n)

def pack4(w):
    words, scales = pack_weight(w, "e2m1")
    return words.reshape(words.shape[0], 128, -1), scales


def unpack4(words, scales):
    return unpack_weight(words.reshape(words.shape[0], 128, -1, 2), scales, "e2m1")


B, N, DIM, HEADS, DIM_HEAD = 2, 512, 1024, 16, 64
INNER = HEADS * DIM_HEAD


def setup_inputs():
    s = mx_kscale(DIM)
    x = bf(np.random.standard_normal((B, N, DIM)) * s)
    w = np.random.standard_normal((3 * INNER, DIM)) / np.sqrt(DIM) / s[None, :]
    words, scales = pack4(np.ascontiguousarray(w.T))
    return {"x": x, "W_words": words, "W_scales": scales}


def reference(x, W_words, W_scales):
    b, n, _ = x.shape
    qkv = mxq(f64(x), 2, "e4m3") @ unpack4(W_words, W_scales)
    q, k, v = np.split(qkv, 3, axis=-1)

    def to_heads(t):
        return t.reshape(b, n, HEADS, DIM_HEAD).transpose(0, 2, 1, 3)

    return to_heads(q), to_heads(k), to_heads(v)

@@ -1,0 +1,122 @@
+from contextlib import ExitStack
+
+import concourse.mybir as mybir
+from concourse.masks import make_identity
+
+F32 = mybir.dt.float32
+BF16 = mybir.dt.bfloat16
+I32 = mybir.dt.int32
+U32 = mybir.dt.uint32
+U8 = mybir.dt.uint8
+FP8X4 = mybir.dt.float8_e4m3fn_x4
+FP4X4 = mybir.dt.float4_e2m1fn_x4
+
+P = 128
+PACK = 4
+K_PASS = P * PACK
+
+BATCH, TOKENS, DIM = 2, 512, 1024
+HEADS, HEAD_DIM = 16, 64
+COLS = 3 * HEADS * HEAD_DIM
+PASSES = DIM // K_PASS
+TILES = BATCH * TOKENS // P
+N_TILE = 512
+GROUPS = COLS // N_TILE
+GROUP_HEADS = N_TILE // HEAD_DIM
+PAIRS = PACK // 2
+
+FLOPS = 2 * BATCH * TOKENS * DIM * COLS
+
+
+def tile_get_qkv_kernel(tc, x, W_words, W_scales, out_0, out_1, out_2):
+    nc = tc.nc
+    parts = [out_0, out_1, out_2]
+
+    with ExitStack() as ctx:
+        keep = ctx.enter_context(tc.tile_pool(name="keep", bufs=1))
+        stage = ctx.enter_context(tc.tile_pool(name="stage", bufs=3))
+        xt_psum = ctx.enter_context(tc.psum_pool(name="xt_psum", bufs=4))
+        acc_psum = ctx.enter_context(tc.psum_pool(name="acc_psum", bufs=4))
+
+        w_planes = keep.tile([P, PASSES, COLS], U8, align_bytes=64)
+        nc.vector.memset(w_planes[:].bitcast(I32), 0)
+
+        ident = keep.tile([P, P], F32)
+        make_identity(nc, ident[:])
+
+        x_by_tile = x.rearrange("b (q j) k -> j q b k", j=TILES)
+        x_rows = []
+        for j in range(TILES):
+            rows = keep.tile([P, DIM], BF16, name="x_rows%d" % j)
+            nc.sync.dma_start(out=rows[:], in_=x_by_tile[j])
+            x_rows.append(rows)
+
+        planes_i32 = w_planes[:].bitcast(I32)
+        scale_rows = W_scales.bitcast(I32).rearrange("g s n -> s g n")
+        for Q in range(2):
+            for r in range(4):
+                nc.sync.dma_start(
+                    out=planes_i32[32 * Q + r : P : 64, :, :],
+                    in_=scale_rows[4 * Q + r : 16 : 8, :, :],
+                )
+
+        words_i32 = W_words.bitcast(I32).rearrange("g p n -> p g n")
+        w_words = []
+        for c in range(GROUPS):
+            words = keep.tile([P, PASSES, 2 * N_TILE], U8, name="w_words%d" % c, align_bytes=64)
+            nc.sync.dma_start(
+                out=words[:].bitcast(I32),
+                in_=words_i32[:, :, c * N_TILE // 2 : (c + 1) * N_TILE // 2],
+            )
+            w_words.append(words)
+
+        x_codes = []
+        x_scales = []
+        for j in range(TILES):
+            x_pairs = x_rows[j][:].bitcast(F32)
+            xt = xt_psum.tile([P, PASSES, PAIRS, P], F32)
+            for g in range(PASSES):
+                for u in range(PAIRS):
+                    nc.tensor.transpose(
+                        xt[:, g, u, :],
+                        x_pairs[:, g * P * PAIRS + u : (g + 1) * P * PAIRS : PAIRS],
+                        ident[:],
+                    )
+            grouped = stage.tile([P, PASSES * P * PACK], BF16, align_bytes=64)
+            nc.scalar.copy(
+                out=grouped[:].bitcast(F32).rearrange("p (g r u) -> p g r u", g=PASSES, u=PAIRS),
+                in_=xt[:].rearrange("p g u r -> p g r u"),
+            )
+            codes = keep.tile([P, PASSES * P], U32, name="x_codes%d" % j, align_bytes=64)
+            scales = keep.tile([P, PASSES * P], U8, name="x_scales%d" % j, align_bytes=64)
+            nc.vector.quantize_mx(out=codes[:].bitcast(FP8X4), scales=scales[:], in_=grouped[:])
+            x_codes.append(codes)
+            x_scales.append(scales)
+
+        for c in range(GROUPS):
+            n_cols = slice(c * N_TILE, (c + 1) * N_TILE)
+            result = keep.tile([P, GROUP_HEADS, TILES, HEAD_DIM], F32, name="result%d" % c)
+            for j in range(TILES):
+                acc = acc_psum.tile([P, N_TILE], F32)
+                for g in range(PASSES):
+                    tokens = slice(g * P, (g + 1) * P)
+                    nc.tensor.matmul_mx(
+                        out=acc[:],
+                        lhsT=x_codes[j][:, tokens].bitcast(FP8X4),
+                        lhsT_scale=x_scales[j][:, tokens],
+                        rhs=w_words[c][:, g, :].bitcast(FP4X4),
+                        rhs_scale=w_planes[:, g, n_cols],
+                        start=(g == 0),
+                        stop=(g == PASSES - 1),
+                    )
+                by_head = acc[:].rearrange("p (h d) -> p h d", d=HEAD_DIM)
+                if j % 2 == 0:
+                    nc.vector.tensor_copy(out=result[:, :, j, :], in_=by_head)
+                else:
+                    nc.scalar.copy(out=result[:, :, j, :], in_=by_head)
+            for i in range(GROUP_HEADS):
+                part, h = divmod(c * GROUP_HEADS + i, HEADS)
+                nc.sync.dma_start(
+                    out=parts[part][:, h, :, :].rearrange("b (q j) d -> q b (j d)", j=TILES),
+                    in_=result[:, i, :, :].rearrange("p j d -> p (j d)"),
+                )

@@ -20,9 +20,13 @@ HEADS, HEAD_DIM = 16, 64
 COLS = 3 * HEADS * HEAD_DIM
 PASSES = DIM // K_PASS
 TILES = BATCH * TOKENS // P
-N_TILE = 512
-GROUPS = COLS // N_TILE
-GROUP_HEADS = N_TILE // HEAD_DIM
+BANK = 512
+LOAD_COLS = 512
+LOADS = COLS // LOAD_COLS
+N_UNIT = 128
+UNITS = COLS // N_UNIT
+UNIT_HEADS = N_UNIT // HEAD_DIM
+BANK_TILES = BANK // N_UNIT
 PAIRS = PACK // 2
 
 FLOPS = 2 * BATCH * TOKENS * DIM * COLS
@@ -62,11 +66,11 @@ def tile_get_qkv_kernel(tc, x, W_words, W_scales, out_0, out_1, out_2):
 
         words_i32 = W_words.bitcast(I32).rearrange("g p n -> p g n")
         w_words = []
-        for c in range(GROUPS):
-            words = keep.tile([P, PASSES, 2 * N_TILE], U8, name="w_words%d" % c, align_bytes=64)
+        for c in range(LOADS):
+            words = keep.tile([P, PASSES, 2 * LOAD_COLS], U8, name="w_words%d" % c, align_bytes=64)
             nc.sync.dma_start(
                 out=words[:].bitcast(I32),
-                in_=words_i32[:, :, c * N_TILE // 2 : (c + 1) * N_TILE // 2],
+                in_=words_i32[:, :, c * LOAD_COLS // 2 : (c + 1) * LOAD_COLS // 2],
             )
             w_words.append(words)
 
@@ -93,29 +97,34 @@ def tile_get_qkv_kernel(tc, x, W_words, W_scales, out_0, out_1, out_2):
             x_codes.append(codes)
             x_scales.append(scales)
 
-        for c in range(GROUPS):
-            n_cols = slice(c * N_TILE, (c + 1) * N_TILE)
-            result = keep.tile([P, GROUP_HEADS, TILES, HEAD_DIM], F32, name="result%d" % c)
-            for j in range(TILES):
-                acc = acc_psum.tile([P, N_TILE], F32)
-                for g in range(PASSES):
-                    tokens = slice(g * P, (g + 1) * P)
-                    nc.tensor.matmul_mx(
-                        out=acc[:],
-                        lhsT=x_codes[j][:, tokens].bitcast(FP8X4),
-                        lhsT_scale=x_scales[j][:, tokens],
-                        rhs=w_words[c][:, g, :].bitcast(FP4X4),
-                        rhs_scale=w_planes[:, g, n_cols],
-                        start=(g == 0),
-                        stop=(g == PASSES - 1),
-                    )
-                by_head = acc[:].rearrange("p (h d) -> p h d", d=HEAD_DIM)
-                if j % 2 == 0:
-                    nc.vector.tensor_copy(out=result[:, :, j, :], in_=by_head)
+        for c in range(UNITS):
+            first_col = c * N_UNIT
+            words = w_words[first_col // LOAD_COLS]
+            word_bytes = slice(2 * (first_col % LOAD_COLS), 2 * (first_col % LOAD_COLS + N_UNIT))
+            result = keep.tile([P, UNIT_HEADS, TILES, HEAD_DIM], F32, name="result%d" % c)
+            for bank in range(TILES // BANK_TILES):
+                acc = acc_psum.tile([P, BANK_TILES, N_UNIT], F32)
+                for i in range(BANK_TILES):
+                    j = bank * BANK_TILES + i
+                    for g in range(PASSES):
+                        tokens = slice(g * P, (g + 1) * P)
+                        nc.tensor.matmul_mx(
+                            out=acc[:, i, :],
+                            lhsT=x_codes[j][:, tokens].bitcast(FP8X4),
+                            lhsT_scale=x_scales[j][:, tokens],
+                            rhs=words[:, g, word_bytes].bitcast(FP4X4),
+                            rhs_scale=w_planes[:, g, first_col : first_col + N_UNIT],
+                            start=(g == 0),
+                            stop=(g == PASSES - 1),
+                        )
+                by_head = acc[:].rearrange("p i (h d) -> p h i d", d=HEAD_DIM)
+                tiles = slice(bank * BANK_TILES, (bank + 1) * BANK_TILES)
+                if bank % 2 == 0:
+                    nc.vector.tensor_copy(out=result[:, :, tiles, :], in_=by_head)
                 else:
-                    nc.scalar.copy(out=result[:, :, j, :], in_=by_head)
-            for i in range(GROUP_HEADS):
-                part, h = divmod(c * GROUP_HEADS + i, HEADS)
+                    nc.scalar.copy(out=result[:, :, tiles, :], in_=by_head)
+            for i in range(UNIT_HEADS):
+                part, h = divmod(c * UNIT_HEADS + i, HEADS)
                 nc.sync.dma_start(
                     out=parts[part][:, h, :, :].rearrange("b (q j) d -> q b (j d)", j=TILES),
                     in_=result[:, i, :, :].rearrange("p j d -> p (j d)"),

@@ -48,21 +48,17 @@ def tile_get_qkv_kernel(tc, x, W_words, W_scales, out_0, out_1, out_2):
         ident = keep.tile([P, P], F32)
         make_identity(nc, ident[:])
 
+        planes_f32 = w_planes[:].bitcast(F32)
+        scale_rows = W_scales.bitcast(F32).rearrange("g s n -> s g n")
+        for r in range(4):
+            nc.gpsimd.dma_start(out=planes_f32[r : P : 32, :, :], in_=scale_rows[r : 16 : 4, :, :])
+
         x_by_tile = x.rearrange("b (q j) k -> j q b k", j=TILES)
         x_rows = []
         for j in range(TILES):
             rows = keep.tile([P, DIM], BF16, name="x_rows%d" % j)
             nc.sync.dma_start(out=rows[:], in_=x_by_tile[j])
             x_rows.append(rows)
-
-        planes_i32 = w_planes[:].bitcast(I32)
-        scale_rows = W_scales.bitcast(I32).rearrange("g s n -> s g n")
-        for Q in range(2):
-            for r in range(4):
-                nc.sync.dma_start(
-                    out=planes_i32[32 * Q + r : P : 64, :, :],
-                    in_=scale_rows[4 * Q + r : 16 : 8, :, :],
-                )
 
         words_i32 = W_words.bitcast(I32).rearrange("g p n -> p g n")
         w_words = []

@@ -20,14 +20,12 @@ HEADS, HEAD_DIM = 16, 64
 COLS = 3 * HEADS * HEAD_DIM
 PASSES = DIM // K_PASS
 TILES = BATCH * TOKENS // P
+PAIRS = PACK // 2
 BANK = 512
-LOAD_COLS = 512
-LOADS = COLS // LOAD_COLS
 N_UNIT = 128
-UNITS = COLS // N_UNIT
 UNIT_HEADS = N_UNIT // HEAD_DIM
 BANK_TILES = BANK // N_UNIT
-PAIRS = PACK // 2
+FIRST_SECTION = 512
 
 FLOPS = 2 * BATCH * TOKENS * DIM * COLS
 
@@ -35,23 +33,23 @@ FLOPS = 2 * BATCH * TOKENS * DIM * COLS
 def tile_get_qkv_kernel(tc, x, W_words, W_scales, out_0, out_1, out_2):
     nc = tc.nc
     parts = [out_0, out_1, out_2]
+    sections = [(0, FIRST_SECTION), (FIRST_SECTION, COLS)]
 
     with ExitStack() as ctx:
+        ctx.enter_context(tc.manual_schedule())
         keep = ctx.enter_context(tc.tile_pool(name="keep", bufs=1))
         stage = ctx.enter_context(tc.tile_pool(name="stage", bufs=3))
         xt_psum = ctx.enter_context(tc.psum_pool(name="xt_psum", bufs=4))
         acc_psum = ctx.enter_context(tc.psum_pool(name="acc_psum", bufs=4))
 
-        w_planes = keep.tile([P, PASSES, COLS], U8, align_bytes=64)
-        nc.vector.memset(w_planes[:].bitcast(I32), 0)
+        w_planes = []
+        for first, end in sections:
+            planes = keep.tile([P, PASSES, end - first], U8, name="w_planes%d" % first, align_bytes=64)
+            nc.vector.memset(planes[:].bitcast(I32), 0)
+            w_planes.append(planes)
 
         ident = keep.tile([P, P], F32)
         make_identity(nc, ident[:])
-
-        planes_f32 = w_planes[:].bitcast(F32)
-        scale_rows = W_scales.bitcast(F32).rearrange("g s n -> s g n")
-        for r in range(4):
-            nc.gpsimd.dma_start(out=planes_f32[r : P : 32, :, :], in_=scale_rows[r : 16 : 4, :, :])
 
         x_by_tile = x.rearrange("b (q j) k -> j q b k", j=TILES)
         x_rows = []
@@ -60,14 +58,17 @@ def tile_get_qkv_kernel(tc, x, W_words, W_scales, out_0, out_1, out_2):
             nc.sync.dma_start(out=rows[:], in_=x_by_tile[j])
             x_rows.append(rows)
 
-        words_i32 = W_words.bitcast(I32).rearrange("g p n -> p g n")
+        scale_rows = W_scales.bitcast(I32).rearrange("g s n -> s g n")
+        word_rows = W_words.bitcast(I32).rearrange("g p n -> p g n")
         w_words = []
-        for c in range(LOADS):
-            words = keep.tile([P, PASSES, 2 * LOAD_COLS], U8, name="w_words%d" % c, align_bytes=64)
-            nc.sync.dma_start(
-                out=words[:].bitcast(I32),
-                in_=words_i32[:, :, c * LOAD_COLS // 2 : (c + 1) * LOAD_COLS // 2],
-            )
+        for planes, (first, end) in zip(w_planes, sections):
+            for r in range(4):
+                nc.sync.dma_start(
+                    out=planes[:].bitcast(I32)[r : P : 32, :, :],
+                    in_=scale_rows[r : 16 : 4, :, first // 4 : end // 4],
+                )
+            words = keep.tile([P, PASSES, 2 * (end - first)], U8, name="w_words%d" % first, align_bytes=64)
+            nc.sync.dma_start(out=words[:].bitcast(I32), in_=word_rows[:, :, first // 2 : end // 2])
             w_words.append(words)
 
         x_codes = []
@@ -93,35 +94,34 @@ def tile_get_qkv_kernel(tc, x, W_words, W_scales, out_0, out_1, out_2):
             x_codes.append(codes)
             x_scales.append(scales)
 
-        for c in range(UNITS):
-            first_col = c * N_UNIT
-            words = w_words[first_col // LOAD_COLS]
-            word_bytes = slice(2 * (first_col % LOAD_COLS), 2 * (first_col % LOAD_COLS + N_UNIT))
-            result = keep.tile([P, UNIT_HEADS, TILES, HEAD_DIM], F32, name="result%d" % c)
-            for bank in range(TILES // BANK_TILES):
-                acc = acc_psum.tile([P, BANK_TILES, N_UNIT], F32)
-                for i in range(BANK_TILES):
-                    j = bank * BANK_TILES + i
-                    for g in range(PASSES):
-                        tokens = slice(g * P, (g + 1) * P)
-                        nc.tensor.matmul_mx(
-                            out=acc[:, i, :],
-                            lhsT=x_codes[j][:, tokens].bitcast(FP8X4),
-                            lhsT_scale=x_scales[j][:, tokens],
-                            rhs=words[:, g, word_bytes].bitcast(FP4X4),
-                            rhs_scale=w_planes[:, g, first_col : first_col + N_UNIT],
-                            start=(g == 0),
-                            stop=(g == PASSES - 1),
-                        )
-                by_head = acc[:].rearrange("p i (h d) -> p h i d", d=HEAD_DIM)
-                tiles = slice(bank * BANK_TILES, (bank + 1) * BANK_TILES)
-                if bank % 2 == 0:
-                    nc.vector.tensor_copy(out=result[:, :, tiles, :], in_=by_head)
-                else:
-                    nc.scalar.copy(out=result[:, :, tiles, :], in_=by_head)
-            for i in range(UNIT_HEADS):
-                part, h = divmod(c * UNIT_HEADS + i, HEADS)
-                nc.sync.dma_start(
-                    out=parts[part][:, h, :, :].rearrange("b (q j) d -> q b (j d)", j=TILES),
-                    in_=result[:, i, :, :].rearrange("p j d -> p (j d)"),
-                )
+        for words, planes, (first, end) in zip(w_words, w_planes, sections):
+            for col in range(first, end, N_UNIT):
+                local = col - first
+                result = keep.tile([P, UNIT_HEADS, TILES, HEAD_DIM], F32, name="result%d" % col)
+                for bank in range(TILES // BANK_TILES):
+                    acc = acc_psum.tile([P, BANK_TILES, N_UNIT], F32)
+                    for i in range(BANK_TILES):
+                        j = bank * BANK_TILES + i
+                        for g in range(PASSES):
+                            tokens = slice(g * P, (g + 1) * P)
+                            nc.tensor.matmul_mx(
+                                out=acc[:, i, :],
+                                lhsT=x_codes[j][:, tokens].bitcast(FP8X4),
+                                lhsT_scale=x_scales[j][:, tokens],
+                                rhs=words[:, g, 2 * local : 2 * (local + N_UNIT)].bitcast(FP4X4),
+                                rhs_scale=planes[:, g, local : local + N_UNIT],
+                                start=(g == 0),
+                                stop=(g == PASSES - 1),
+                            )
+                    by_head = acc[:].rearrange("p i (h d) -> p h i d", d=HEAD_DIM)
+                    tiles = slice(bank * BANK_TILES, (bank + 1) * BANK_TILES)
+                    if bank % 2 == 0:
+                        nc.vector.tensor_copy(out=result[:, :, tiles, :], in_=by_head)
+                    else:
+                        nc.scalar.copy(out=result[:, :, tiles, :], in_=by_head)
+                for k in range(UNIT_HEADS):
+                    part, h = divmod(col // HEAD_DIM + k, HEADS)
+                    nc.sync.dma_start(
+                        out=parts[part][:, h, :, :].rearrange("b (q j) d -> q b (j d)", j=TILES),
+                        in_=result[:, k, :, :].rearrange("p j d -> p (j d)"),
+                    )

@@ -36,7 +36,6 @@ def tile_get_qkv_kernel(tc, x, W_words, W_scales, out_0, out_1, out_2):
     sections = [(0, FIRST_SECTION), (FIRST_SECTION, COLS)]
 
     with ExitStack() as ctx:
-        ctx.enter_context(tc.manual_schedule())
         keep = ctx.enter_context(tc.tile_pool(name="keep", bufs=1))
         stage = ctx.enter_context(tc.tile_pool(name="stage", bufs=3))
         xt_psum = ctx.enter_context(tc.psum_pool(name="xt_psum", bufs=4))

@@ -26,6 +26,7 @@ N_UNIT = 128
 UNIT_HEADS = N_UNIT // HEAD_DIM
 BANK_TILES = BANK // N_UNIT
 FIRST_SECTION = 512
+X_CHUNK = 2
 
 FLOPS = 2 * BATCH * TOKENS * DIM * COLS
 
@@ -50,11 +51,11 @@ def tile_get_qkv_kernel(tc, x, W_words, W_scales, out_0, out_1, out_2):
         ident = keep.tile([P, P], F32)
         make_identity(nc, ident[:])
 
-        x_by_tile = x.rearrange("b (q j) k -> j q b k", j=TILES)
+        x_by_chunk = x.rearrange("b (q c i) k -> c q b (i k)", c=TILES // X_CHUNK, i=X_CHUNK)
         x_rows = []
-        for j in range(TILES):
-            rows = keep.tile([P, DIM], BF16, name="x_rows%d" % j)
-            nc.sync.dma_start(out=rows[:], in_=x_by_tile[j])
+        for c in range(TILES // X_CHUNK):
+            rows = keep.tile([P, X_CHUNK * DIM], BF16, name="x_rows%d" % c)
+            nc.sync.dma_start(out=rows[:], in_=x_by_chunk[c])
             x_rows.append(rows)
 
         scale_rows = W_scales.bitcast(I32).rearrange("g s n -> s g n")
@@ -73,7 +74,8 @@ def tile_get_qkv_kernel(tc, x, W_words, W_scales, out_0, out_1, out_2):
         x_codes = []
         x_scales = []
         for j in range(TILES):
-            x_pairs = x_rows[j][:].bitcast(F32)
+            i = j % X_CHUNK
+            x_pairs = x_rows[j // X_CHUNK][:, i * DIM : (i + 1) * DIM].bitcast(F32)
             xt = xt_psum.tile([P, PASSES, PAIRS, P], F32)
             for g in range(PASSES):
                 for u in range(PAIRS):

@@ -27,6 +27,8 @@ UNIT_HEADS = N_UNIT // HEAD_DIM
 BANK_TILES = BANK // N_UNIT
 FIRST_SECTION = 512
 X_CHUNK = 2
+SPLIT_FIRST = 2
+SPLIT_LAST = 0
 
 FLOPS = 2 * BATCH * TOKENS * DIM * COLS
 
@@ -95,34 +97,55 @@ def tile_get_qkv_kernel(tc, x, W_words, W_scales, out_0, out_1, out_2):
             x_codes.append(codes)
             x_scales.append(scales)
 
+        units = []
         for words, planes, (first, end) in zip(w_words, w_planes, sections):
             for col in range(first, end, N_UNIT):
-                local = col - first
-                result = keep.tile([P, UNIT_HEADS, TILES, HEAD_DIM], F32, name="result%d" % col)
-                for bank in range(TILES // BANK_TILES):
-                    acc = acc_psum.tile([P, BANK_TILES, N_UNIT], F32)
-                    for i in range(BANK_TILES):
-                        j = bank * BANK_TILES + i
-                        for g in range(PASSES):
-                            tokens = slice(g * P, (g + 1) * P)
-                            nc.tensor.matmul_mx(
-                                out=acc[:, i, :],
-                                lhsT=x_codes[j][:, tokens].bitcast(FP8X4),
-                                lhsT_scale=x_scales[j][:, tokens],
-                                rhs=words[:, g, 2 * local : 2 * (local + N_UNIT)].bitcast(FP4X4),
-                                rhs_scale=planes[:, g, local : local + N_UNIT],
-                                start=(g == 0),
-                                stop=(g == PASSES - 1),
-                            )
-                    by_head = acc[:].rearrange("p i (h d) -> p h i d", d=HEAD_DIM)
-                    tiles = slice(bank * BANK_TILES, (bank + 1) * BANK_TILES)
-                    if bank % 2 == 0:
-                        nc.vector.tensor_copy(out=result[:, :, tiles, :], in_=by_head)
-                    else:
-                        nc.scalar.copy(out=result[:, :, tiles, :], in_=by_head)
-                for k in range(UNIT_HEADS):
-                    part, h = divmod(col // HEAD_DIM + k, HEADS)
-                    nc.sync.dma_start(
-                        out=parts[part][:, h, :, :].rearrange("b (q j) d -> q b (j d)", j=TILES),
-                        in_=result[:, k, :, :].rearrange("p j d -> p (j d)"),
+                units.append((words, planes, col - first, col))
+        results = {}
+
+        def half_unit(n, bank):
+            words, planes, local, col = units[n]
+            if bank == 0:
+                results[n] = keep.tile([P, UNIT_HEADS, TILES, HEAD_DIM], F32, name="result%d" % col)
+            acc = acc_psum.tile([P, BANK_TILES, N_UNIT], F32, name="acc")
+            for i in range(BANK_TILES):
+                j = bank * BANK_TILES + i
+                for g in range(PASSES):
+                    tokens = slice(g * P, (g + 1) * P)
+                    nc.tensor.matmul_mx(
+                        out=acc[:, i, :],
+                        lhsT=x_codes[j][:, tokens].bitcast(FP8X4),
+                        lhsT_scale=x_scales[j][:, tokens],
+                        rhs=words[:, g, 2 * local : 2 * (local + N_UNIT)].bitcast(FP4X4),
+                        rhs_scale=planes[:, g, local : local + N_UNIT],
+                        start=(g == 0),
+                        stop=(g == PASSES - 1),
                     )
+            by_head = acc[:].rearrange("p i (h d) -> p h i d", d=HEAD_DIM)
+            tiles = slice(bank * BANK_TILES, (bank + 1) * BANK_TILES)
+            if bank % 2 == 0:
+                nc.vector.tensor_copy(out=results[n][:, :, tiles, :], in_=by_head)
+            else:
+                nc.scalar.copy(out=results[n][:, :, tiles, :], in_=by_head)
+
+        def store(n, j0, j1):
+            for k in range(UNIT_HEADS):
+                part, h = divmod(units[n][3] // HEAD_DIM + k, HEADS)
+                by_tile = parts[part][:, h, :, :].rearrange("b (q j) d -> q b j d", j=TILES)
+                nc.sync.dma_start(
+                    out=by_tile[:, :, j0:j1, :].rearrange("q b j d -> q b (j d)"),
+                    in_=results[n][:, k, j0:j1, :].rearrange("p j d -> p (j d)"),
+                )
+
+        for bank in range(TILES // BANK_TILES):
+            for n in range(SPLIT_FIRST):
+                half_unit(n, bank)
+                store(n, bank * BANK_TILES, (bank + 1) * BANK_TILES)
+        for n in range(SPLIT_FIRST, len(units) - SPLIT_LAST):
+            for bank in range(TILES // BANK_TILES):
+                half_unit(n, bank)
+            store(n, 0, TILES)
+        for n in range(len(units) - SPLIT_LAST, len(units)):
+            for bank in range(TILES // BANK_TILES):
+                half_unit(n, bank)
+                store(n, bank * BANK_TILES, (bank + 1) * BANK_TILES)

from contextlib import ExitStack

import concourse.mybir as mybir
from concourse.masks import make_identity

F32 = mybir.dt.float32
BF16 = mybir.dt.bfloat16
I32 = mybir.dt.int32
U32 = mybir.dt.uint32
U8 = mybir.dt.uint8
FP8X4 = mybir.dt.float8_e4m3fn_x4
FP4X4 = mybir.dt.float4_e2m1fn_x4

P = 128
PACK = 4
K_PASS = P * PACK

BATCH, TOKENS, DIM = 2, 512, 1024
HEADS, HEAD_DIM = 16, 64
COLS = 3 * HEADS * HEAD_DIM
PASSES = DIM // K_PASS
TILES = BATCH * TOKENS // P
PAIRS = PACK // 2
BANK = 512
N_UNIT = 128
UNIT_HEADS = N_UNIT // HEAD_DIM
BANK_TILES = BANK // N_UNIT
FIRST_SECTION = 512
X_CHUNK = 2
SPLIT_FIRST = 2
SPLIT_LAST = 0

FLOPS = 2 * BATCH * TOKENS * DIM * COLS


def tile_get_qkv_kernel(tc, x, W_words, W_scales, out_0, out_1, out_2):
    nc = tc.nc
    parts = [out_0, out_1, out_2]
    sections = [(0, FIRST_SECTION), (FIRST_SECTION, COLS)]

    with ExitStack() as ctx:
        keep = ctx.enter_context(tc.tile_pool(name="keep", bufs=1))
        stage = ctx.enter_context(tc.tile_pool(name="stage", bufs=3))
        xt_psum = ctx.enter_context(tc.psum_pool(name="xt_psum", bufs=4))
        acc_psum = ctx.enter_context(tc.psum_pool(name="acc_psum", bufs=4))

        w_planes = []
        for first, end in sections:
            planes = keep.tile([P, PASSES, end - first], U8, name="w_planes%d" % first, align_bytes=64)
            nc.vector.memset(planes[:].bitcast(I32), 0)
            w_planes.append(planes)

        ident = keep.tile([P, P], F32)
        make_identity(nc, ident[:])

        x_by_chunk = x.rearrange("b (q c i) k -> c q b (i k)", c=TILES // X_CHUNK, i=X_CHUNK)
        x_rows = []
        for c in range(TILES // X_CHUNK):
            rows = keep.tile([P, X_CHUNK * DIM], BF16, name="x_rows%d" % c)
            nc.sync.dma_start(out=rows[:], in_=x_by_chunk[c])
            x_rows.append(rows)

        scale_rows = W_scales.bitcast(I32).rearrange("g s n -> s g n")
        word_rows = W_words.bitcast(I32).rearrange("g p n -> p g n")
        w_words = []
        for planes, (first, end) in zip(w_planes, sections):
            for r in range(4):
                nc.sync.dma_start(
                    out=planes[:].bitcast(I32)[r : P : 32, :, :],
                    in_=scale_rows[r : 16 : 4, :, first // 4 : end // 4],
                )
            words = keep.tile([P, PASSES, 2 * (end - first)], U8, name="w_words%d" % first, align_bytes=64)
            nc.sync.dma_start(out=words[:].bitcast(I32), in_=word_rows[:, :, first // 2 : end // 2])
            w_words.append(words)

        x_codes = []
        x_scales = []
        for j in range(TILES):
            i = j % X_CHUNK
            x_pairs = x_rows[j // X_CHUNK][:, i * DIM : (i + 1) * DIM].bitcast(F32)
            xt = xt_psum.tile([P, PASSES, PAIRS, P], F32)
            for g in range(PASSES):
                for u in range(PAIRS):
                    nc.tensor.transpose(
                        xt[:, g, u, :],
                        x_pairs[:, g * P * PAIRS + u : (g + 1) * P * PAIRS : PAIRS],
                        ident[:],
                    )
            grouped = stage.tile([P, PASSES * P * PACK], BF16, align_bytes=64)
            nc.scalar.copy(
                out=grouped[:].bitcast(F32).rearrange("p (g r u) -> p g r u", g=PASSES, u=PAIRS),
                in_=xt[:].rearrange("p g u r -> p g r u"),
            )
            codes = keep.tile([P, PASSES * P], U32, name="x_codes%d" % j, align_bytes=64)
            scales = keep.tile([P, PASSES * P], U8, name="x_scales%d" % j, align_bytes=64)
            nc.vector.quantize_mx(out=codes[:].bitcast(FP8X4), scales=scales[:], in_=grouped[:])
            x_codes.append(codes)
            x_scales.append(scales)

        units = []
        for words, planes, (first, end) in zip(w_words, w_planes, sections):
            for col in range(first, end, N_UNIT):
                units.append((words, planes, col - first, col))
        results = {}

        def half_unit(n, bank):
            words, planes, local, col = units[n]
            if bank == 0:
                results[n] = keep.tile([P, UNIT_HEADS, TILES, HEAD_DIM], F32, name="result%d" % col)
            acc = acc_psum.tile([P, BANK_TILES, N_UNIT], F32, name="acc")
            for i in range(BANK_TILES):
                j = bank * BANK_TILES + i
                for g in range(PASSES):
                    tokens = slice(g * P, (g + 1) * P)
                    nc.tensor.matmul_mx(
                        out=acc[:, i, :],
                        lhsT=x_codes[j][:, tokens].bitcast(FP8X4),
                        lhsT_scale=x_scales[j][:, tokens],
                        rhs=words[:, g, 2 * local : 2 * (local + N_UNIT)].bitcast(FP4X4),
                        rhs_scale=planes[:, g, local : local + N_UNIT],
                        start=(g == 0),
                        stop=(g == PASSES - 1),
                    )
            by_head = acc[:].rearrange("p i (h d) -> p h i d", d=HEAD_DIM)
            tiles = slice(bank * BANK_TILES, (bank + 1) * BANK_TILES)
            if bank % 2 == 0:
                nc.vector.tensor_copy(out=results[n][:, :, tiles, :], in_=by_head)
            else:
                nc.scalar.copy(out=results[n][:, :, tiles, :], in_=by_head)

        def store(n, j0, j1):
            for k in range(UNIT_HEADS):
                part, h = divmod(units[n][3] // HEAD_DIM + k, HEADS)
                by_tile = parts[part][:, h, :, :].rearrange("b (q j) d -> q b j d", j=TILES)
                nc.sync.dma_start(
                    out=by_tile[:, :, j0:j1, :].rearrange("q b j d -> q b (j d)"),
                    in_=results[n][:, k, j0:j1, :].rearrange("p j d -> p (j d)"),
                )

        for bank in range(TILES // BANK_TILES):
            for n in range(SPLIT_FIRST):
                half_unit(n, bank)
                store(n, bank * BANK_TILES, (bank + 1) * BANK_TILES)
        for n in range(SPLIT_FIRST, len(units) - SPLIT_LAST):
            for bank in range(TILES // BANK_TILES):
                half_unit(n, bank)
            store(n, 0, TILES)
        for n in range(len(units) - SPLIT_LAST, len(units)):
            for bank in range(TILES // BANK_TILES):
                half_unit(n, bank)
                store(n, bank * BANK_TILES, (bank + 1) * BANK_TILES)
